import numpy as np
import ml_dtypes


def mxq(x, axis, fmt="e4m3"):
    dtype, down = {"e4m3": (ml_dtypes.float8_e4m3fn, 7), "e5m2": (ml_dtypes.float8_e5m2, 14)}[fmt]
    v = np.moveaxis(np.asarray(x, np.float32).astype(ml_dtypes.bfloat16).astype(np.float64), axis, -1)
    blocks = v.reshape(v.shape[:-1] + (-1, 32))
    amax = np.abs(blocks).max(-1, keepdims=True)
    byte = np.maximum(np.where(amax > 0, np.frexp(amax)[1] - 1 + 127, 0) - down, 1)
    scale = np.exp2(byte - 127.0)
    codes = (blocks / scale).astype(np.float32).astype(dtype).astype(np.float64)
    return np.moveaxis((codes * scale).reshape(v.shape), -1, axis)


WIDE = False


def mx_kscale(k):
    if not WIDE:
        return np.ones(k)
    levels = np.array([10, -10, 5, -5, 0])
    a = np.random.permutation(np.resize(levels, k // 512 * 4)).reshape(k // 512, 4)
    idx = np.arange(k)
    return np.exp2(a[idx // 512, idx % 128 // 32])


BF16 = ml_dtypes.bfloat16


def bf(x):
    return np.asarray(x, np.float32).astype(BF16)


def f64(x):
    return np.asarray(x).astype(np.float64)


B, IN_DIM, R_IN, R_OUT = 128, 2048, 2048, 2048
HIDDEN = R_IN + R_OUT
BASELINE_THRE = 0.1
BETA = 1.8
R_M = 3.0
DT = 1.0


def sigmoid(v):
    return 1.0 / (1.0 + np.exp(-v))


def setup_inputs():
    s = mx_kscale(IN_DIM)
    return {
        "x_t": bf(np.random.standard_normal((B, IN_DIM)) * s),
        "spk_t": bf(np.random.random((B, HIDDEN)) < 0.3),
        "mem_t_in": bf(np.random.standard_normal((B, R_IN))),
        "b_t_in": bf(np.random.random((B, R_IN))),
        "W_x2in": bf(np.random.standard_normal((R_IN, IN_DIM)) / np.sqrt(IN_DIM) / s[None, :]),
        "b_x2in": bf(np.random.standard_normal(R_IN) * 0.5),
        "W_rec4in": bf(np.random.standard_normal((R_IN, R_IN)) * 1.5 / np.sqrt(R_IN)),
        "b_rec4in": bf(np.random.standard_normal(R_IN) * 0.5),
        "W_out2in": bf(np.random.standard_normal((R_IN, R_OUT)) * 1.5 / np.sqrt(R_OUT)),
        "b_out2in": bf(np.random.standard_normal(R_IN) * 0.5),
        "tau_adp_in": bf(1.5 + 0.5 * np.random.standard_normal(R_IN)),
        "tau_m_in": bf(2.0 + 0.5 * np.random.standard_normal(R_IN)),
    }


def reference(x_t, spk_t, mem_t_in, b_t_in, W_x2in, b_x2in, W_rec4in, b_rec4in, W_out2in, b_out2in, tau_adp_in, tau_m_in):
    spk = f64(spk_t)
    spk_out = spk[:, :R_OUT]
    spk_in = spk[:, R_OUT:]
    x = (mxq(f64(x_t), 1, "e4m3") @ mxq(f64(W_x2in), 1, "e4m3").T) + f64(b_x2in)
    rec = (mxq(spk_in, 1, "e4m3") @ mxq(f64(W_rec4in), 1, "e4m3").T) + f64(b_rec4in)
    fbk = (mxq(spk_out, 1, "e4m3") @ mxq(f64(W_out2in), 1, "e4m3").T) + f64(b_out2in)
    r_in_ = x + rec + fbk
    tau_m_s = sigmoid(f64(tau_m_in))
    tau_adp_s = sigmoid(f64(tau_adp_in))
    b = tau_adp_s * f64(b_t_in) + (1.0 - tau_adp_s) * spk_in
    new_thre = BASELINE_THRE + BETA * b
    mem = f64(mem_t_in) * tau_m_s + (1.0 - tau_m_s) * R_M * r_in_ - new_thre * spk_in * DT
    return mem

@@ -1,0 +1,325 @@
+from contextlib import ExitStack
+
+import concourse.bass as bass
+import concourse.mybir as mybir
+import concourse.tile as tile
+from concourse.masks import make_identity
+
+F32 = mybir.dt.float32
+BF16 = mybir.dt.bfloat16
+U32 = mybir.dt.uint32
+U8 = mybir.dt.uint8
+I32 = mybir.dt.int32
+FP8X4 = mybir.dt.float8_e4m3fn_x4
+ALU = mybir.AluOpType
+ACT = mybir.ActivationFunctionType
+
+P = 128
+KDIM = 2048
+ODIM = 2048
+OT = 512
+N_OT = ODIM // OT
+N_W = 3
+PASSES_W = KDIM // 512
+N_CHUNK = N_OT * N_W
+N_PASS = N_CHUNK * PASSES_W
+FLOPS = 2 * 128 * 3 * KDIM * ODIM
+
+MANUAL = True
+RP = 2
+LAG_Q = 1
+LAG_M = 2
+NBUF_W = 5
+VEC_EVERY = 16
+KAPPA = 0.1 / 1.8
+
+
+def tile_snnlayer_pa_kernel(
+    tc,
+    x_t,
+    spk_t,
+    mem_t_in,
+    b_t_in,
+    W_x2in,
+    b_x2in,
+    W_rec4in,
+    b_rec4in,
+    W_out2in,
+    b_out2in,
+    tau_adp_in,
+    tau_m_in,
+    out,
+):
+    nc = tc.nc
+    weights = [W_x2in, W_rec4in, W_out2in]
+    with ExitStack() as ctx:
+        if MANUAL:
+            ctx.enter_context(tc.manual_schedule())
+        keep = ctx.enter_context(tc.tile_pool(name="keep", bufs=1))
+        wpool = ctx.enter_context(tc.tile_pool(name="wraw", bufs=NBUF_W))
+        gpool = ctx.enter_context(tc.tile_pool(name="grp", bufs=6))
+        tpool = ctx.enter_context(tc.tile_pool(name="tmp", bufs=2))
+        psum = ctx.enter_context(tc.psum_pool(name="psum", bufs=1))
+
+        ident = keep.tile([P, P], F32, name="ident")
+        make_identity(nc, ident[:])
+        vrow = keep.tile([P, ODIM], BF16, name="vrow")
+        nc.vector.memset(vrow[:].bitcast(I32), 0)
+        sel = keep.tile([P, 3, P], BF16, name="sel")
+        nc.vector.memset(sel[:].bitcast(I32), 0)
+        nc.vector.memset(sel[0:3, 0, :], 1.0)
+        nc.vector.memset(sel[32:33, 1, :], 1.0)
+        nc.vector.memset(sel[64:65, 2, :], 1.0)
+
+        def row(v):
+            return v.rearrange("(o n) -> o n", o=1)
+
+        nc.scalar.dma_start(out=vrow[32:33, :], in_=row(tau_m_in))
+        nc.scalar.dma_start(out=vrow[64:65, :], in_=row(tau_adp_in))
+        nc.scalar.dma_start(out=vrow[0:1, :], in_=row(b_x2in))
+        nc.scalar.dma_start(out=vrow[1:2, :], in_=row(b_rec4in))
+        nc.scalar.dma_start(out=vrow[2:3, :], in_=row(b_out2in))
+
+        x_sb = keep.tile([P, KDIM], BF16, name="x_sb")
+        nc.sync.dma_start(out=x_sb[:], in_=x_t)
+        spk_sb = keep.tile([P, 2 * KDIM], BF16, name="spk_sb")
+        nc.sync.dma_start(out=spk_sb[:], in_=spk_t)
+        mem_sb = keep.tile([P, ODIM], BF16, name="mem_sb")
+        bt_sb = keep.tile([P, ODIM], BF16, name="bt_sb")
+
+        wraw = {}
+
+        def load_w(ci, pieces):
+            n, w = divmod(ci, N_W)
+            t = wpool.tile([P, 4, KDIM], BF16, name="wraw%d" % ci, tag="wraw")
+            wraw[ci] = t
+            src = weights[w][OT * n : OT * (n + 1), :].rearrange("(c t) k -> c t k", t=4)
+            step = KDIM // pieces
+            for i in range(pieces):
+                nc.sync.dma_start(
+                    out=t[:, :, i * step : (i + 1) * step],
+                    in_=src[:, :, i * step : (i + 1) * step],
+                )
+
+        load_w(0, 4)
+        load_w(1, 1)
+        nc.sync.dma_start(out=mem_sb[:], in_=mem_t_in)
+        nc.sync.dma_start(out=bt_sb[:], in_=b_t_in)
+        for ci in range(2, NBUF_W):
+            load_w(ci, 1)
+
+        a_sb = keep.tile([P, ODIM], F32, name="a_sb")
+        p_sb = keep.tile([P, ODIM], F32, name="p_sb")
+        a3_sb = keep.tile([P, ODIM], F32, name="a3_sb")
+        b_sb = keep.tile([P, ODIM], F32, name="b_sb")
+
+        def bank(name):
+            return psum.tile([P, 512], F32, name=name, tag="tp", bufs=6)
+
+        def spread(n):
+            sl = slice(OT * n, OT * (n + 1))
+            tm = bank("tm%d" % n)
+            nc.tensor.matmul(tm[:], lhsT=sel[:, 1, :], rhs=vrow[:, sl], start=True, stop=True)
+            nc.scalar.activation(out=a_sb[:, sl], in_=tm[:], func=ACT.Sigmoid)
+            tp_ = bank("tq%d" % n)
+            nc.tensor.matmul(tp_[:], lhsT=sel[:, 2, :], rhs=vrow[:, sl], start=True, stop=True)
+            nc.scalar.activation(out=p_sb[:, sl], in_=tp_[:], func=ACT.Sigmoid)
+            bs = bank("bs%d" % n)
+            nc.tensor.matmul(bs[:], lhsT=sel[:, 0, :], rhs=vrow[:, sl], start=True, stop=True)
+            nc.vector.tensor_scalar(
+                out=a3_sb[:, sl], in0=a_sb[:, sl], scalar1=-1.0, scalar2=1.0, op0=ALU.mult, op1=ALU.add
+            )
+            nc.vector.scalar_tensor_tensor(
+                out=b_sb[:, sl], in0=bs[:], scalar=3.0, in1=a3_sb[:, sl], op0=ALU.mult, op1=ALU.mult
+            )
+
+        a_grp = keep.tile([P, 12 * 512], BF16, name="a_grp", align_bytes=64)
+        a_codes = keep.tile([P, 12 * P], U32, name="a_codes", align_bytes=64)
+        a_scales = keep.tile([P, 12 * P], U8, name="a_scales", align_bytes=64)
+        x_w = x_sb[:].bitcast(F32)
+        spk_w = spk_sb[:].bitcast(F32)
+        a_grp_w = a_grp[:].bitcast(F32).rearrange("p (a b u) -> p a b u", b=P, u=2)
+
+        def act_words(a):
+            w, g = divmod(a, PASSES_W)
+            if w == 0:
+                return x_w, 256 * g
+            if w == 1:
+                return spk_w, 1024 + 256 * g
+            return spk_w, 256 * g
+
+        def act_bank(i):
+            bk = bank("ab%d" % i)
+            for j in range(2):
+                src, off = act_words(2 * i + j)
+                for u in range(2):
+                    q = 2 * j + u
+                    nc.tensor.transpose(
+                        bk[:, P * q : P * (q + 1)], src[:, off + P * u : off + P * (u + 1)], ident[:]
+                    )
+            nc.scalar.copy(
+                out=a_grp_w[:, 2 * i : 2 * i + 2, :, :],
+                in_=bk[:].rearrange("p (a u b) -> p a b u", a=2, u=2),
+            )
+
+        def act_quant(w):
+            nc.vector.quantize_mx(
+                out=a_codes[:, 512 * w : 512 * (w + 1)].bitcast(FP8X4),
+                scales=a_scales[:, 512 * w : 512 * (w + 1)],
+                in_=a_grp[:, 2048 * w : 2048 * (w + 1)],
+            )
+
+        spread(0)
+        spread(1)
+        act_bank(0)
+        act_bank(1)
+        spread(2)
+        spread(3)
+        act_quant(0)
+        for i in range(2, 6):
+            act_bank(i)
+        act_quant(1)
+        act_quant(2)
+
+        fill = []
+
+        def bterm(n):
+            sl = slice(OT * n, OT * (n + 1))
+            s = spk_sb[:, KDIM + OT * n : KDIM + OT * (n + 1)]
+            box = {}
+
+            def op0():
+                box["t1"] = tpool.tile([P, OT], F32, name="t1_%d" % n, tag="t1")
+                nc.vector.tensor_tensor(out=box["t1"][:], in0=bt_sb[:, sl], in1=s, op=ALU.subtract)
+
+            def op1():
+                nc.vector.tensor_tensor(out=box["t1"][:], in0=box["t1"][:], in1=p_sb[:, sl], op=ALU.mult)
+
+            def op2():
+                nc.vector.tensor_tensor(out=box["t1"][:], in0=box["t1"][:], in1=s, op=ALU.add)
+
+            def op3():
+                nc.vector.scalar_tensor_tensor(
+                    out=box["t1"][:], in0=box["t1"][:], scalar=KAPPA, in1=s, op0=ALU.add, op1=ALU.mult
+                )
+
+            def op4():
+                box["t2"] = tpool.tile([P, OT], F32, name="t2_%d" % n, tag="t2")
+                nc.vector.tensor_tensor(out=box["t2"][:], in0=mem_sb[:, sl], in1=a_sb[:, sl], op=ALU.mult)
+
+            def op5():
+                nc.vector.tensor_tensor(out=b_sb[:, sl], in0=b_sb[:, sl], in1=box["t2"][:], op=ALU.add)
+
+            def op6():
+                nc.vector.scalar_tensor_tensor(
+                    out=b_sb[:, sl], in0=box["t1"][:], scalar=-1.8, in1=b_sb[:, sl], op0=ALU.mult, op1=ALU.add
+                )
+
+            return [op0, op4, op1, op5, op2, op3, op6]
+
+        for n in range(N_OT):
+            fill.extend(bterm(n))
+
+        grp = {}
+        codes = {}
+        scales = {}
+        acc = {}
+        n_bank = [0]
+
+        def transposes(q):
+            ci, g = divmod(q, PASSES_W)
+            ww = wraw[ci][:].bitcast(F32)
+            gt = gpool.tile([P, 2048], BF16, name="grp%d" % q, tag="grp", align_bytes=64)
+            grp[q] = gt
+            gw = gt[:].bitcast(F32).rearrange("p (j u) -> p j u", u=2)
+            todo = []
+            for h in range(2):
+                bk = bank("wb%d_%d" % (q, h))
+                for u in range(2):
+                    for tt in range(2):
+                        col = 256 * u + P * tt
+                        off = 256 * g + P * u
+                        nc.tensor.transpose(
+                            bk[:, col : col + P], ww[:, 2 * h + tt, off : off + P], ident[:]
+                        )
+                todo.append((bk, gw[:, 256 * h : 256 * (h + 1), :]))
+            return todo
+
+        def copies(todo):
+            for bk, dst in todo:
+                src = bk[:].rearrange("p (u j) -> p j u", u=2)
+                n_bank[0] += 1
+                if VEC_EVERY and n_bank[0] % VEC_EVERY == 0:
+                    nc.vector.tensor_copy(out=dst, in_=src)
+                else:
+                    nc.scalar.copy(out=dst, in_=src)
+
+        def quant(q):
+            cd = gpool.tile([P, 512], U32, name="cd%d" % q, tag="cd", align_bytes=64)
+            sc = gpool.tile([P, 512], U8, name="sc%d" % q, tag="sc", align_bytes=64)
+            codes[q] = cd
+            scales[q] = sc
+            nc.vector.quantize_mx(out=cd[:].bitcast(FP8X4), scales=sc[:], in_=grp[q][:])
+
+        def mx(q):
+            n, r = divmod(q, N_W * PASSES_W)
+            if r == 0:
+                acc[n] = psum.tile([P, OT], F32, name="acc%d" % n, tag="acc", bufs=2)
+            nc.tensor.matmul_mx(
+                out=acc[n][:],
+                lhsT=a_codes[:, P * r : P * (r + 1)].bitcast(FP8X4),
+                lhsT_scale=a_scales[:, P * r : P * (r + 1)],
+                rhs=codes[q][:].bitcast(FP8X4),
+                rhs_scale=scales[q][:],
+                start=(r == 0),
+                stop=(r == N_W * PASSES_W - 1),
+            )
+
+        def epilogue(n):
+            sl = slice(OT * n, OT * (n + 1))
+            res = tpool.tile([P, OT], F32, name="res%d" % n, tag="res")
+            nc.vector.scalar_tensor_tensor(
+                out=res[:].rearrange("p (c t) -> p c t", t=4),
+                in0=acc[n][:].rearrange("p (t c) -> p c t", t=4),
+                scalar=3.0,
+                in1=a3_sb[:, sl].rearrange("p (c t) -> p c t", t=4),
+                op0=ALU.mult,
+                op1=ALU.mult,
+            )
+            nc.vector.tensor_tensor(out=res[:], in0=res[:], in1=b_sb[:, sl], op=ALU.add)
+            nc.sync.dma_start(out=out[:, sl], in_=res[:])
+
+        n_round = N_PASS // RP
+        next_load = NBUF_W
+        per_tile = N_W * PASSES_W
+        pending_epi = []
+        fill_pos = 0
+        for r in range(n_round + LAG_M + 1):
+            todo = []
+            if r < n_round:
+                for q in range(RP * r, RP * (r + 1)):
+                    todo.extend(transposes(q))
+                copies(todo)
+            rq = r - LAG_Q
+            if 0 <= rq < n_round:
+                for q in range(RP * rq, RP * (rq + 1)):
+                    quant(q)
+            for n in pending_epi:
+                epilogue(n)
+            pending_epi = []
+            rm = r - LAG_M
+            if 0 <= rm < n_round:
+                for q in range(RP * rm, RP * (rm + 1)):
+                    mx(q)
+                    if q % per_tile == per_tile - 1:
+                        pending_epi.append(q // per_tile)
+            if r < n_round and (RP * (r + 1)) % PASSES_W == 0 and next_load < N_CHUNK:
+                load_w(next_load, 4 if next_load == N_CHUNK - 1 else 1)
+                next_load += 1
+            k = 2 if r % 2 == 0 else 1
+            for i in range(k):
+                if fill_pos < len(fill):
+                    fill[fill_pos]()
+                    fill_pos += 1
+        for n in pending_epi:
+            epilogue(n)

@@ -1,8 +1,6 @@
 from contextlib import ExitStack
 
-import concourse.bass as bass
 import concourse.mybir as mybir
-import concourse.tile as tile
 from concourse.masks import make_identity
 
 F32 = mybir.dt.float32
@@ -17,20 +15,23 @@ ACT = mybir.ActivationFunctionType
 P = 128
 KDIM = 2048
 ODIM = 2048
-OT = 512
+OT = 256
+TR = OT // P
 N_OT = ODIM // OT
 N_W = 3
 PASSES_W = KDIM // 512
 N_CHUNK = N_OT * N_W
-N_PASS = N_CHUNK * PASSES_W
+FW = 512
 FLOPS = 2 * 128 * 3 * KDIM * ODIM
 
 MANUAL = True
-RP = 2
 LAG_Q = 1
-LAG_M = 2
-NBUF_W = 5
-VEC_EVERY = 16
+LAG_M = 3
+NBUF_W = 10
+GB = 10
+VEC_FROM = 12
+HEAD_FILL = 4
+FILL_PER_ROUND = 2
 KAPPA = 0.1 / 1.8
 
 
@@ -51,25 +52,30 @@ def tile_snnlayer_pa_kernel(
     out,
 ):
     nc = tc.nc
-    weights = [W_x2in, W_rec4in, W_out2in]
+    weights = [W_rec4in, W_out2in, W_x2in]
     with ExitStack() as ctx:
         if MANUAL:
             ctx.enter_context(tc.manual_schedule())
         keep = ctx.enter_context(tc.tile_pool(name="keep", bufs=1))
         wpool = ctx.enter_context(tc.tile_pool(name="wraw", bufs=NBUF_W))
-        gpool = ctx.enter_context(tc.tile_pool(name="grp", bufs=6))
+        gpool = ctx.enter_context(tc.tile_pool(name="grp", bufs=GB))
         tpool = ctx.enter_context(tc.tile_pool(name="tmp", bufs=2))
         psum = ctx.enter_context(tc.psum_pool(name="psum", bufs=1))
 
-        ident = keep.tile([P, P], F32, name="ident")
-        make_identity(nc, ident[:])
+        warm = keep.tile([P, 2], F32, name="warm")
+        nc.vector.memset(warm[:], 0.0)
+        nc.scalar.activation(out=warm[:, 1:2], in_=warm[:, 0:1], func=ACT.Sigmoid)
         vrow = keep.tile([P, ODIM], BF16, name="vrow")
         nc.vector.memset(vrow[:].bitcast(I32), 0)
         sel = keep.tile([P, 3, P], BF16, name="sel")
         nc.vector.memset(sel[:].bitcast(I32), 0)
-        nc.vector.memset(sel[0:3, 0, :], 1.0)
+        nc.vector.memset(sel[0:3, 0, :], -3.0)
         nc.vector.memset(sel[32:33, 1, :], 1.0)
         nc.vector.memset(sel[64:65, 2, :], 1.0)
+        ident = keep.tile([P, P], F32, name="ident")
+        make_identity(nc, ident[:])
+        identb = keep.tile([P, P], BF16, name="identb")
+        make_identity(nc, identb[:])
 
         def row(v):
             return v.rearrange("(o n) -> o n", o=1)
@@ -80,35 +86,30 @@ def tile_snnlayer_pa_kernel(
         nc.scalar.dma_start(out=vrow[1:2, :], in_=row(b_rec4in))
         nc.scalar.dma_start(out=vrow[2:3, :], in_=row(b_out2in))
 
-        x_sb = keep.tile([P, KDIM], BF16, name="x_sb")
-        nc.sync.dma_start(out=x_sb[:], in_=x_t)
         spk_sb = keep.tile([P, 2 * KDIM], BF16, name="spk_sb")
-        nc.sync.dma_start(out=spk_sb[:], in_=spk_t)
-        mem_sb = keep.tile([P, ODIM], BF16, name="mem_sb")
         bt_sb = keep.tile([P, ODIM], BF16, name="bt_sb")
+        mem_sb = keep.tile([P, ODIM], BF16, name="mem_sb")
+        x_sb = keep.tile([P, KDIM], BF16, name="x_sb")
+        nc.sync.dma_start(out=spk_sb[:], in_=spk_t)
+        nc.sync.dma_start(out=bt_sb[:], in_=b_t_in)
+        nc.sync.dma_start(out=mem_sb[:], in_=mem_t_in)
 
         wraw = {}
 
-        def load_w(ci, pieces):
+        def load_w(ci):
             n, w = divmod(ci, N_W)
-            t = wpool.tile([P, 4, KDIM], BF16, name="wraw%d" % ci, tag="wraw")
+            t = wpool.tile([P, TR, KDIM], BF16, name="wraw%d" % ci, tag="wraw")
             wraw[ci] = t
-            src = weights[w][OT * n : OT * (n + 1), :].rearrange("(c t) k -> c t k", t=4)
-            step = KDIM // pieces
-            for i in range(pieces):
-                nc.sync.dma_start(
-                    out=t[:, :, i * step : (i + 1) * step],
-                    in_=src[:, :, i * step : (i + 1) * step],
-                )
+            nc.sync.dma_start(
+                out=t[:], in_=weights[w][OT * n : OT * (n + 1), :].rearrange("(c t) k -> c t k", t=TR)
+            )
 
-        load_w(0, 4)
-        load_w(1, 1)
-        nc.sync.dma_start(out=mem_sb[:], in_=mem_t_in)
-        nc.sync.dma_start(out=bt_sb[:], in_=b_t_in)
+        load_w(0)
+        load_w(1)
+        nc.sync.dma_start(out=x_sb[:], in_=x_t)
         for ci in range(2, NBUF_W):
-            load_w(ci, 1)
+            load_w(ci)
 
-        a_sb = keep.tile([P, ODIM], F32, name="a_sb")
         p_sb = keep.tile([P, ODIM], F32, name="p_sb")
         a3_sb = keep.tile([P, ODIM], F32, name="a3_sb")
         b_sb = keep.tile([P, ODIM], F32, name="b_sb")
@@ -116,22 +117,21 @@ def tile_snnlayer_pa_kernel(
         def bank(name):
             return psum.tile([P, 512], F32, name=name, tag="tp", bufs=6)
 
-        def spread(n):
-            sl = slice(OT * n, OT * (n + 1))
-            tm = bank("tm%d" % n)
+        def taus(f):
+            sl = slice(FW * f, FW * (f + 1))
+            tm = bank("tm%d" % f)
             nc.tensor.matmul(tm[:], lhsT=sel[:, 1, :], rhs=vrow[:, sl], start=True, stop=True)
-            nc.scalar.activation(out=a_sb[:, sl], in_=tm[:], func=ACT.Sigmoid)
-            tp_ = bank("tq%d" % n)
-            nc.tensor.matmul(tp_[:], lhsT=sel[:, 2, :], rhs=vrow[:, sl], start=True, stop=True)
-            nc.scalar.activation(out=p_sb[:, sl], in_=tp_[:], func=ACT.Sigmoid)
-            bs = bank("bs%d" % n)
-            nc.tensor.matmul(bs[:], lhsT=sel[:, 0, :], rhs=vrow[:, sl], start=True, stop=True)
-            nc.vector.tensor_scalar(
-                out=a3_sb[:, sl], in0=a_sb[:, sl], scalar1=-1.0, scalar2=1.0, op0=ALU.mult, op1=ALU.add
-            )
-            nc.vector.scalar_tensor_tensor(
-                out=b_sb[:, sl], in0=bs[:], scalar=3.0, in1=a3_sb[:, sl], op0=ALU.mult, op1=ALU.mult
-            )
+            nc.scalar.activation(out=a3_sb[:, sl], in_=tm[:], func=ACT.Sigmoid, scale=-1.0)
+            tq = bank("tq%d" % f)
+            nc.tensor.matmul(tq[:], lhsT=sel[:, 2, :], rhs=vrow[:, sl], start=True, stop=True)
+            nc.scalar.activation(out=p_sb[:, sl], in_=tq[:], func=ACT.Sigmoid)
+
+        def mem_minus_bias(f):
+            sl = slice(FW * f, FW * (f + 1))
+            xb = bank("xb%d" % f)
+            nc.tensor.matmul(xb[:], lhsT=sel[:, 0, :], rhs=vrow[:, sl], start=True, stop=False)
+            nc.tensor.matmul(xb[:], lhsT=identb[:], rhs=mem_sb[:, sl], start=False, stop=True)
+            nc.vector.tensor_tensor(out=b_sb[:, sl], in0=xb[:], in1=a3_sb[:, sl], op=ALU.mult)
 
         a_grp = keep.tile([P, 12 * 512], BF16, name="a_grp", align_bytes=64)
         a_codes = keep.tile([P, 12 * P], U32, name="a_codes", align_bytes=64)
@@ -143,10 +143,10 @@ def tile_snnlayer_pa_kernel(
         def act_words(a):
             w, g = divmod(a, PASSES_W)
             if w == 0:
-                return x_w, 256 * g
-            if w == 1:
                 return spk_w, 1024 + 256 * g
-            return spk_w, 256 * g
+            if w == 1:
+                return spk_w, 256 * g
+            return x_w, 256 * g
 
         def act_bank(i):
             bk = bank("ab%d" % i)
@@ -157,7 +157,7 @@ def tile_snnlayer_pa_kernel(
                     nc.tensor.transpose(
                         bk[:, P * q : P * (q + 1)], src[:, off + P * u : off + P * (u + 1)], ident[:]
                     )
-            nc.scalar.copy(
+            nc.vector.tensor_copy(
                 out=a_grp_w[:, 2 * i : 2 * i + 2, :, :],
                 in_=bk[:].rearrange("p (a u b) -> p a b u", a=2, u=2),
             )
@@ -169,157 +169,160 @@ def tile_snnlayer_pa_kernel(
                 in_=a_grp[:, 2048 * w : 2048 * (w + 1)],
             )
 
-        spread(0)
-        spread(1)
-        act_bank(0)
-        act_bank(1)
-        spread(2)
-        spread(3)
-        act_quant(0)
-        for i in range(2, 6):
-            act_bank(i)
-        act_quant(1)
-        act_quant(2)
-
-        fill = []
-
-        def bterm(n):
-            sl = slice(OT * n, OT * (n + 1))
-            s = spk_sb[:, KDIM + OT * n : KDIM + OT * (n + 1)]
+        def bterm(f):
+            sl = slice(FW * f, FW * (f + 1))
+            s = spk_sb[:, KDIM + FW * f : KDIM + FW * (f + 1)]
             box = {}
 
-            def op0():
-                box["t1"] = tpool.tile([P, OT], F32, name="t1_%d" % n, tag="t1")
+            def w0():
+                box["t1"] = tpool.tile([P, FW], F32, name="t1_%d" % f, tag="t1")
                 nc.vector.tensor_tensor(out=box["t1"][:], in0=bt_sb[:, sl], in1=s, op=ALU.subtract)
 
-            def op1():
+            def b1():
+                nc.vector.tensor_tensor(out=b_sb[:, sl], in0=mem_sb[:, sl], in1=b_sb[:, sl], op=ALU.subtract)
+
+            def w1():
                 nc.vector.tensor_tensor(out=box["t1"][:], in0=box["t1"][:], in1=p_sb[:, sl], op=ALU.mult)
 
-            def op2():
+            def w2():
                 nc.vector.tensor_tensor(out=box["t1"][:], in0=box["t1"][:], in1=s, op=ALU.add)
 
-            def op3():
+            def w3():
                 nc.vector.scalar_tensor_tensor(
                     out=box["t1"][:], in0=box["t1"][:], scalar=KAPPA, in1=s, op0=ALU.add, op1=ALU.mult
                 )
 
-            def op4():
-                box["t2"] = tpool.tile([P, OT], F32, name="t2_%d" % n, tag="t2")
-                nc.vector.tensor_tensor(out=box["t2"][:], in0=mem_sb[:, sl], in1=a_sb[:, sl], op=ALU.mult)
-
-            def op5():
-                nc.vector.tensor_tensor(out=b_sb[:, sl], in0=b_sb[:, sl], in1=box["t2"][:], op=ALU.add)
-
-            def op6():
+            def b2():
                 nc.vector.scalar_tensor_tensor(
                     out=b_sb[:, sl], in0=box["t1"][:], scalar=-1.8, in1=b_sb[:, sl], op0=ALU.mult, op1=ALU.add
                 )
 
-            return [op0, op4, op1, op5, op2, op3, op6]
+            return [w0, b1, w1, w2, w3, b2]
 
-        for n in range(N_OT):
-            fill.extend(bterm(n))
+        fill = []
+        for f in range(ODIM // FW):
+            fill.extend(bterm(f))
 
         grp = {}
         codes = {}
         scales = {}
         acc = {}
-        n_bank = [0]
 
-        def transposes(q):
-            ci, g = divmod(q, PASSES_W)
+        def transposes(ci, gp):
             ww = wraw[ci][:].bitcast(F32)
-            gt = gpool.tile([P, 2048], BF16, name="grp%d" % q, tag="grp", align_bytes=64)
-            grp[q] = gt
+            gt = gpool.tile([P, 2048], BF16, name="grp%d_%d" % (ci, gp), tag="grp", bufs=6, align_bytes=64)
+            grp[(ci, gp)] = gt
             gw = gt[:].bitcast(F32).rearrange("p (j u) -> p j u", u=2)
             todo = []
             for h in range(2):
-                bk = bank("wb%d_%d" % (q, h))
+                g = 2 * gp + h
+                bk = bank("wb%d_%d" % (ci, g))
                 for u in range(2):
-                    for tt in range(2):
+                    for tt in range(TR):
                         col = 256 * u + P * tt
                         off = 256 * g + P * u
-                        nc.tensor.transpose(
-                            bk[:, col : col + P], ww[:, 2 * h + tt, off : off + P], ident[:]
-                        )
+                        nc.tensor.transpose(bk[:, col : col + P], ww[:, tt, off : off + P], ident[:])
                 todo.append((bk, gw[:, 256 * h : 256 * (h + 1), :]))
             return todo
 
-        def copies(todo):
-            for bk, dst in todo:
-                src = bk[:].rearrange("p (u j) -> p j u", u=2)
-                n_bank[0] += 1
-                if VEC_EVERY and n_bank[0] % VEC_EVERY == 0:
-                    nc.vector.tensor_copy(out=dst, in_=src)
-                else:
-                    nc.scalar.copy(out=dst, in_=src)
+        def copy_out(item, on_vector):
+            bk, dst = item
+            src = bk[:].rearrange("p (u j) -> p j u", u=2)
+            if on_vector:
+                nc.vector.tensor_copy(out=dst, in_=src)
+            else:
+                nc.scalar.copy(out=dst, in_=src)
 
-        def quant(q):
-            cd = gpool.tile([P, 512], U32, name="cd%d" % q, tag="cd", align_bytes=64)
-            sc = gpool.tile([P, 512], U8, name="sc%d" % q, tag="sc", align_bytes=64)
-            codes[q] = cd
-            scales[q] = sc
-            nc.vector.quantize_mx(out=cd[:].bitcast(FP8X4), scales=sc[:], in_=grp[q][:])
+        def quant(ci, gp):
+            cd = gpool.tile([P, 512], U32, name="cd%d_%d" % (ci, gp), tag="cd", align_bytes=64)
+            sc = gpool.tile([P, 512], U8, name="sc%d_%d" % (ci, gp), tag="sc", align_bytes=64)
+            codes[(ci, gp)] = cd
+            scales[(ci, gp)] = sc
+            nc.vector.quantize_mx(out=cd[:].bitcast(FP8X4), scales=sc[:], in_=grp[(ci, gp)][:])
 
-        def mx(q):
-            n, r = divmod(q, N_W * PASSES_W)
-            if r == 0:
+        def mx(ci):
+            n, w = divmod(ci, N_W)
+            if w == 0:
                 acc[n] = psum.tile([P, OT], F32, name="acc%d" % n, tag="acc", bufs=2)
-            nc.tensor.matmul_mx(
-                out=acc[n][:],
-                lhsT=a_codes[:, P * r : P * (r + 1)].bitcast(FP8X4),
-                lhsT_scale=a_scales[:, P * r : P * (r + 1)],
-                rhs=codes[q][:].bitcast(FP8X4),
-                rhs_scale=scales[q][:],
-                start=(r == 0),
-                stop=(r == N_W * PASSES_W - 1),
-            )
+            for g in range(PASSES_W):
+                gp, h = divmod(g, 2)
+                r = w * PASSES_W + g
+                nc.tensor.matmul_mx(
+                    out=acc[n][:],
+                    lhsT=a_codes[:, P * r : P * (r + 1)].bitcast(FP8X4),
+                    lhsT_scale=a_scales[:, P * r : P * (r + 1)],
+                    rhs=codes[(ci, gp)][:, 256 * h : 256 * (h + 1)].bitcast(FP8X4),
+                    rhs_scale=scales[(ci, gp)][:, 256 * h : 256 * (h + 1)],
+                    start=(r == 0),
+                    stop=(r == N_W * PASSES_W - 1),
+                )
 
         def epilogue(n):
             sl = slice(OT * n, OT * (n + 1))
-            res = tpool.tile([P, OT], F32, name="res%d" % n, tag="res")
+            res = tpool.tile([P, OT], F32, name="res%d" % n, tag="res", bufs=3)
             nc.vector.scalar_tensor_tensor(
-                out=res[:].rearrange("p (c t) -> p c t", t=4),
-                in0=acc[n][:].rearrange("p (t c) -> p c t", t=4),
+                out=res[:].rearrange("p (c t) -> p c t", t=TR),
+                in0=acc[n][:].rearrange("p (t c) -> p c t", t=TR),
                 scalar=3.0,
-                in1=a3_sb[:, sl].rearrange("p (c t) -> p c t", t=4),
+                in1=a3_sb[:, sl].rearrange("p (c t) -> p c t", t=TR),
                 op0=ALU.mult,
                 op1=ALU.mult,
             )
             nc.vector.tensor_tensor(out=res[:], in0=res[:], in1=b_sb[:, sl], op=ALU.add)
             nc.sync.dma_start(out=out[:, sl], in_=res[:])
 
-        n_round = N_PASS // RP
-        next_load = NBUF_W
-        per_tile = N_W * PASSES_W
-        pending_epi = []
+        taus(0)
+        taus(1)
+        taus(2)
+        act_bank(0)
+        act_bank(1)
+        taus(3)
+        act_bank(2)
+        act_bank(3)
+        mem_minus_bias(0)
+        mem_minus_bias(1)
+        act_quant(0)
+        act_quant(1)
+        mem_minus_bias(2)
+        mem_minus_bias(3)
         fill_pos = 0
-        for r in range(n_round + LAG_M + 1):
-            todo = []
-            if r < n_round:
-                for q in range(RP * r, RP * (r + 1)):
-                    todo.extend(transposes(q))
-                copies(todo)
+        for i in range(HEAD_FILL):
+            fill[fill_pos]()
+            fill_pos += 1
+
+        next_load = NBUF_W
+        pending_epi = []
+        for r in range(N_CHUNK + LAG_M + 1):
+            late = []
+            if r < N_CHUNK:
+                todo = transposes(r, 0) + transposes(r, 1)
+                for i in range(4):
+                    if r >= VEC_FROM and i == 3:
+                        late.append(todo[i])
+                    else:
+                        copy_out(todo[i], False)
+            if r == 1:
+                act_bank(4)
+                act_bank(5)
+                act_quant(2)
             rq = r - LAG_Q
-            if 0 <= rq < n_round:
-                for q in range(RP * rq, RP * (rq + 1)):
-                    quant(q)
+            if 0 <= rq < N_CHUNK:
+                quant(rq, 0)
+                quant(rq, 1)
+            for item in late:
+                copy_out(item, True)
             for n in pending_epi:
                 epilogue(n)
             pending_epi = []
             rm = r - LAG_M
-            if 0 <= rm < n_round:
-                for q in range(RP * rm, RP * (rm + 1)):
-                    mx(q)
-                    if q % per_tile == per_tile - 1:
-                        pending_epi.append(q // per_tile)
-            if r < n_round and (RP * (r + 1)) % PASSES_W == 0 and next_load < N_CHUNK:
-                load_w(next_load, 4 if next_load == N_CHUNK - 1 else 1)
+            if 0 <= rm < N_CHUNK:
+                mx(rm)
+                if rm % N_W == N_W - 1:
+                    pending_epi.append(rm // N_W)
+            if r < N_CHUNK and next_load < N_CHUNK:
+                load_w(next_load)
                 next_load += 1
-            k = 2 if r % 2 == 0 else 1
-            for i in range(k):
+            for i in range(FILL_PER_ROUND):
                 if fill_pos < len(fill):
                     fill[fill_pos]()
                     fill_pos += 1
-        for n in pending_epi:
-            epilogue(n)

@@ -28,10 +28,8 @@ MANUAL = True
 LAG_Q = 1
 LAG_M = 3
 NBUF_W = 10
-GB = 10
-VEC_FROM = 12
-HEAD_FILL = 4
-FILL_PER_ROUND = 2
+GB = 6
+HEAD_FILL = 2
 KAPPA = 0.1 / 1.8
 
 
@@ -208,21 +206,20 @@ def tile_snnlayer_pa_kernel(
         scales = {}
         acc = {}
 
-        def transposes(ci, gp):
+        def transposes(ci):
             ww = wraw[ci][:].bitcast(F32)
-            gt = gpool.tile([P, 2048], BF16, name="grp%d_%d" % (ci, gp), tag="grp", bufs=6, align_bytes=64)
-            grp[(ci, gp)] = gt
+            gt = gpool.tile([P, 4096], BF16, name="grp%d" % ci, tag="grp", bufs=4, align_bytes=64)
+            grp[ci] = gt
             gw = gt[:].bitcast(F32).rearrange("p (j u) -> p j u", u=2)
             todo = []
-            for h in range(2):
-                g = 2 * gp + h
+            for g in range(PASSES_W):
                 bk = bank("wb%d_%d" % (ci, g))
                 for u in range(2):
                     for tt in range(TR):
                         col = 256 * u + P * tt
                         off = 256 * g + P * u
                         nc.tensor.transpose(bk[:, col : col + P], ww[:, tt, off : off + P], ident[:])
-                todo.append((bk, gw[:, 256 * h : 256 * (h + 1), :]))
+                todo.append((bk, gw[:, 256 * g : 256 * (g + 1), :]))
             return todo
 
         def copy_out(item, on_vector):
@@ -233,43 +230,49 @@ def tile_snnlayer_pa_kernel(
             else:
                 nc.scalar.copy(out=dst, in_=src)
 
-        def quant(ci, gp):
-            cd = gpool.tile([P, 512], U32, name="cd%d_%d" % (ci, gp), tag="cd", align_bytes=64)
-            sc = gpool.tile([P, 512], U8, name="sc%d_%d" % (ci, gp), tag="sc", align_bytes=64)
-            codes[(ci, gp)] = cd
-            scales[(ci, gp)] = sc
-            nc.vector.quantize_mx(out=cd[:].bitcast(FP8X4), scales=sc[:], in_=grp[(ci, gp)][:])
+        def quant(ci):
+            cd = gpool.tile([P, 1024], U32, name="cd%d" % ci, tag="cd", align_bytes=64)
+            sc = gpool.tile([P, 1024], U8, name="sc%d" % ci, tag="sc", align_bytes=64)
+            codes[ci] = cd
+            scales[ci] = sc
+            nc.vector.quantize_mx(out=cd[:].bitcast(FP8X4), scales=sc[:], in_=grp[ci][:])
 
         def mx(ci):
             n, w = divmod(ci, N_W)
             if w == 0:
                 acc[n] = psum.tile([P, OT], F32, name="acc%d" % n, tag="acc", bufs=2)
             for g in range(PASSES_W):
-                gp, h = divmod(g, 2)
                 r = w * PASSES_W + g
                 nc.tensor.matmul_mx(
                     out=acc[n][:],
                     lhsT=a_codes[:, P * r : P * (r + 1)].bitcast(FP8X4),
                     lhsT_scale=a_scales[:, P * r : P * (r + 1)],
-                    rhs=codes[(ci, gp)][:, 256 * h : 256 * (h + 1)].bitcast(FP8X4),
-                    rhs_scale=scales[(ci, gp)][:, 256 * h : 256 * (h + 1)],
+                    rhs=codes[ci][:, 256 * g : 256 * (g + 1)].bitcast(FP8X4),
+                    rhs_scale=scales[ci][:, 256 * g : 256 * (g + 1)],
                     start=(r == 0),
                     stop=(r == N_W * PASSES_W - 1),
                 )
 
-        def epilogue(n):
+        res = {}
+
+        def scale_sums(n):
+            m, h = divmod(n, 2)
+            if h == 0:
+                res[m] = tpool.tile([P, 2 * OT], F32, name="res%d" % m, tag="res", bufs=2)
             sl = slice(OT * n, OT * (n + 1))
-            res = tpool.tile([P, OT], F32, name="res%d" % n, tag="res", bufs=3)
             nc.vector.scalar_tensor_tensor(
-                out=res[:].rearrange("p (c t) -> p c t", t=TR),
+                out=res[m][:, OT * h : OT * (h + 1)].rearrange("p (c t) -> p c t", t=TR),
                 in0=acc[n][:].rearrange("p (t c) -> p c t", t=TR),
                 scalar=3.0,
                 in1=a3_sb[:, sl].rearrange("p (c t) -> p c t", t=TR),
                 op0=ALU.mult,
                 op1=ALU.mult,
             )
-            nc.vector.tensor_tensor(out=res[:], in0=res[:], in1=b_sb[:, sl], op=ALU.add)
-            nc.sync.dma_start(out=out[:, sl], in_=res[:])
+
+        def finish(m):
+            sl = slice(2 * OT * m, 2 * OT * (m + 1))
+            nc.vector.tensor_tensor(out=res[m][:], in0=res[m][:], in1=b_sb[:, sl], op=ALU.add)
+            nc.sync.dma_start(out=out[:, sl], in_=res[m][:])
 
         taus(0)
         taus(1)
@@ -291,38 +294,32 @@ def tile_snnlayer_pa_kernel(
             fill_pos += 1
 
         next_load = NBUF_W
-        pending_epi = []
+        pending = []
         for r in range(N_CHUNK + LAG_M + 1):
-            late = []
             if r < N_CHUNK:
-                todo = transposes(r, 0) + transposes(r, 1)
-                for i in range(4):
-                    if r >= VEC_FROM and i == 3:
-                        late.append(todo[i])
-                    else:
-                        copy_out(todo[i], False)
+                for item in transposes(r):
+                    copy_out(item, False)
             if r == 1:
                 act_bank(4)
                 act_bank(5)
                 act_quant(2)
             rq = r - LAG_Q
             if 0 <= rq < N_CHUNK:
-                quant(rq, 0)
-                quant(rq, 1)
-            for item in late:
-                copy_out(item, True)
-            for n in pending_epi:
-                epilogue(n)
-            pending_epi = []
+                quant(rq)
+            for n in pending:
+                scale_sums(n)
+            if fill_pos < len(fill):
+                fill[fill_pos]()
+                fill_pos += 1
+            for n in pending:
+                if n % 2 == 1:
+                    finish(n // 2)
+            pending = []
             rm = r - LAG_M
             if 0 <= rm < N_CHUNK:
                 mx(rm)
                 if rm % N_W == N_W - 1:
-                    pending_epi.append(rm // N_W)
+                    pending.append(rm // N_W)
             if r < N_CHUNK and next_load < N_CHUNK:
                 load_w(next_load)
                 next_load += 1
-            for i in range(FILL_PER_ROUND):
-                if fill_pos < len(fill):
-                    fill[fill_pos]()
-                    fill_pos += 1

@@ -29,7 +29,8 @@ LAG_Q = 1
 LAG_M = 3
 NBUF_W = 10
 GB = 6
-HEAD_FILL = 2
+FILL_FROM = 5
+FILL_TWO = 10
 KAPPA = 0.1 / 1.8
 
 
@@ -88,24 +89,31 @@ def tile_snnlayer_pa_kernel(
         bt_sb = keep.tile([P, ODIM], BF16, name="bt_sb")
         mem_sb = keep.tile([P, ODIM], BF16, name="mem_sb")
         x_sb = keep.tile([P, KDIM], BF16, name="x_sb")
-        nc.sync.dma_start(out=spk_sb[:], in_=spk_t)
-        nc.sync.dma_start(out=bt_sb[:], in_=b_t_in)
-        nc.sync.dma_start(out=mem_sb[:], in_=mem_t_in)
 
         wraw = {}
 
-        def load_w(ci):
+        def load_w(ci, parts=1):
             n, w = divmod(ci, N_W)
             t = wpool.tile([P, TR, KDIM], BF16, name="wraw%d" % ci, tag="wraw")
             wraw[ci] = t
-            nc.sync.dma_start(
-                out=t[:], in_=weights[w][OT * n : OT * (n + 1), :].rearrange("(c t) k -> c t k", t=TR)
-            )
+            for h in range(parts):
+                ks = slice(KDIM // parts * h, KDIM // parts * (h + 1))
+                nc.sync.dma_start(
+                    out=t[:, :, ks],
+                    in_=weights[w][OT * n : OT * (n + 1), ks].rearrange("(c t) k -> c t k", t=TR),
+                )
 
-        load_w(0)
+        load_w(0, 2)
+        nc.sync.dma_start(out=spk_sb[:, KDIM:], in_=spk_t[:, KDIM:])
         load_w(1)
+        nc.sync.dma_start(out=spk_sb[:, :KDIM], in_=spk_t[:, :KDIM])
+        load_w(2)
         nc.sync.dma_start(out=x_sb[:], in_=x_t)
-        for ci in range(2, NBUF_W):
+        load_w(3)
+        nc.sync.dma_start(out=mem_sb[:], in_=mem_t_in)
+        load_w(4)
+        nc.sync.dma_start(out=bt_sb[:], in_=b_t_in)
+        for ci in range(5, NBUF_W):
             load_w(ci)
 
         p_sb = keep.tile([P, ODIM], F32, name="p_sb")
@@ -195,7 +203,10 @@ def tile_snnlayer_pa_kernel(
                     out=b_sb[:, sl], in0=box["t1"][:], scalar=-1.8, in1=b_sb[:, sl], op0=ALU.mult, op1=ALU.add
                 )
 
-            return [w0, b1, w1, w2, w3, b2]
+            def mb():
+                mem_minus_bias(f)
+
+            return [mb, b1, w0, w1, w2, w3, b2]
 
         fill = []
         for f in range(ODIM // FW):
@@ -274,24 +285,9 @@ def tile_snnlayer_pa_kernel(
             nc.vector.tensor_tensor(out=res[m][:], in0=res[m][:], in1=b_sb[:, sl], op=ALU.add)
             nc.sync.dma_start(out=out[:, sl], in_=res[m][:])
 
-        taus(0)
-        taus(1)
-        taus(2)
-        act_bank(0)
-        act_bank(1)
-        taus(3)
-        act_bank(2)
-        act_bank(3)
-        mem_minus_bias(0)
-        mem_minus_bias(1)
-        act_quant(0)
-        act_quant(1)
-        mem_minus_bias(2)
-        mem_minus_bias(3)
-        fill_pos = 0
-        for i in range(HEAD_FILL):
-            fill[fill_pos]()
-            fill_pos += 1
+        def next_fill():
+            if fill:
+                fill.pop(0)()
 
         next_load = NBUF_W
         pending = []
@@ -299,18 +295,22 @@ def tile_snnlayer_pa_kernel(
             if r < N_CHUNK:
                 for item in transposes(r):
                     copy_out(item, False)
-            if r == 1:
-                act_bank(4)
-                act_bank(5)
-                act_quant(2)
+            if r < 3:
+                act_bank(2 * r)
+                act_bank(2 * r + 1)
+            if r < 4:
+                taus(r)
+            if 1 <= r < 4:
+                act_quant(r - 1)
+            if FILL_FROM <= r <= FILL_TWO:
+                next_fill()
             rq = r - LAG_Q
             if 0 <= rq < N_CHUNK:
                 quant(rq)
             for n in pending:
                 scale_sums(n)
-            if fill_pos < len(fill):
-                fill[fill_pos]()
-                fill_pos += 1
+            if FILL_FROM <= r:
+                next_fill()
             for n in pending:
                 if n % 2 == 1:
                     finish(n // 2)

@@ -25,12 +25,12 @@ FW = 512
 FLOPS = 2 * 128 * 3 * KDIM * ODIM
 
 MANUAL = True
-LAG_Q = 1
 LAG_M = 3
+LAST_PARTS = 4
 NBUF_W = 10
 GB = 6
 FILL_FROM = 5
-FILL_TWO = 10
+MB_ROUND = [4, 8, 12, 16]
 KAPPA = 0.1 / 1.8
 
 
@@ -92,6 +92,8 @@ def tile_snnlayer_pa_kernel(
 
         wraw = {}
 
+        LAST = N_CHUNK - 1
+
         def load_w(ci, parts=1):
             n, w = divmod(ci, N_W)
             t = wpool.tile([P, TR, KDIM], BF16, name="wraw%d" % ci, tag="wraw")
@@ -132,12 +134,14 @@ def tile_snnlayer_pa_kernel(
             nc.tensor.matmul(tq[:], lhsT=sel[:, 2, :], rhs=vrow[:, sl], start=True, stop=True)
             nc.scalar.activation(out=p_sb[:, sl], in_=tq[:], func=ACT.Sigmoid)
 
+        xbank = {}
+
         def mem_minus_bias(f):
             sl = slice(FW * f, FW * (f + 1))
             xb = bank("xb%d" % f)
             nc.tensor.matmul(xb[:], lhsT=sel[:, 0, :], rhs=vrow[:, sl], start=True, stop=False)
             nc.tensor.matmul(xb[:], lhsT=identb[:], rhs=mem_sb[:, sl], start=False, stop=True)
-            nc.vector.tensor_tensor(out=b_sb[:, sl], in0=xb[:], in1=a3_sb[:, sl], op=ALU.mult)
+            xbank[f] = xb
 
         a_grp = keep.tile([P, 12 * 512], BF16, name="a_grp", align_bytes=64)
         a_codes = keep.tile([P, 12 * P], U32, name="a_codes", align_bytes=64)
@@ -204,11 +208,13 @@ def tile_snnlayer_pa_kernel(
                 )
 
             def mb():
-                mem_minus_bias(f)
+                nc.vector.tensor_tensor(out=b_sb[:, sl], in0=xbank[f][:], in1=a3_sb[:, sl], op=ALU.mult)
 
-            return [mb, b1, w0, w1, w2, w3, b2]
+            mb_v.append(mb)
+            return [b1, w0, w1, w2, w3, b2]
 
         fill = []
+        mb_v = []
         for f in range(ODIM // FW):
             fill.extend(bterm(f))
 
@@ -217,36 +223,39 @@ def tile_snnlayer_pa_kernel(
         scales = {}
         acc = {}
 
-        def transposes(ci):
+        wbank = {}
+
+        def transposes(ci, g):
             ww = wraw[ci][:].bitcast(F32)
-            gt = gpool.tile([P, 4096], BF16, name="grp%d" % ci, tag="grp", bufs=4, align_bytes=64)
-            grp[ci] = gt
-            gw = gt[:].bitcast(F32).rearrange("p (j u) -> p j u", u=2)
-            todo = []
-            for g in range(PASSES_W):
-                bk = bank("wb%d_%d" % (ci, g))
-                for u in range(2):
-                    for tt in range(TR):
-                        col = 256 * u + P * tt
-                        off = 256 * g + P * u
-                        nc.tensor.transpose(bk[:, col : col + P], ww[:, tt, off : off + P], ident[:])
-                todo.append((bk, gw[:, 256 * g : 256 * (g + 1), :]))
-            return todo
+            bk = bank("wb%d_%d" % (ci, g))
+            for u in range(2):
+                for tt in range(TR):
+                    col = 256 * u + P * tt
+                    off = 256 * g + P * u
+                    nc.tensor.transpose(bk[:, col : col + P], ww[:, tt, off : off + P], ident[:])
+            wbank[ci, g] = bk
 
-        def copy_out(item, on_vector):
-            bk, dst = item
-            src = bk[:].rearrange("p (u j) -> p j u", u=2)
-            if on_vector:
-                nc.vector.tensor_copy(out=dst, in_=src)
-            else:
-                nc.scalar.copy(out=dst, in_=src)
+        def copy_out(ci, g):
+            if ci not in grp:
+                gt = gpool.tile([P, 4096], BF16, name="grp%d" % ci, tag="grp", bufs=4, align_bytes=64)
+                grp[ci] = gt
+            gw = grp[ci][:].bitcast(F32).rearrange("p (j u) -> p j u", u=2)
+            dst = gw[:, 256 * g : 256 * (g + 1), :]
+            src = wbank[ci, g][:].rearrange("p (u j) -> p j u", u=2)
+            nc.scalar.copy(out=dst, in_=src)
 
-        def quant(ci):
-            cd = gpool.tile([P, 1024], U32, name="cd%d" % ci, tag="cd", align_bytes=64)
-            sc = gpool.tile([P, 1024], U8, name="sc%d" % ci, tag="sc", align_bytes=64)
-            codes[ci] = cd
-            scales[ci] = sc
-            nc.vector.quantize_mx(out=cd[:].bitcast(FP8X4), scales=sc[:], in_=grp[ci][:])
+        def quant(ci, g0=0, g1=PASSES_W):
+            if ci not in codes:
+                cd = gpool.tile([P, 1024], U32, name="cd%d" % ci, tag="cd", align_bytes=64)
+                sc = gpool.tile([P, 1024], U8, name="sc%d" % ci, tag="sc", align_bytes=64)
+                codes[ci] = cd
+                scales[ci] = sc
+            ws = slice(256 * g0, 256 * g1)
+            nc.vector.quantize_mx(
+                out=codes[ci][:, ws].bitcast(FP8X4),
+                scales=scales[ci][:, ws],
+                in_=grp[ci][:, 1024 * g0 : 1024 * g1],
+            )
 
         def mx(ci):
             n, w = divmod(ci, N_W)
@@ -269,7 +278,7 @@ def tile_snnlayer_pa_kernel(
         def scale_sums(n):
             m, h = divmod(n, 2)
             if h == 0:
-                res[m] = tpool.tile([P, 2 * OT], F32, name="res%d" % m, tag="res", bufs=2)
+                res[m] = tpool.tile([P, 2 * OT], F32, name="res%d" % m, tag="res", bufs=4)
             sl = slice(OT * n, OT * (n + 1))
             nc.vector.scalar_tensor_tensor(
                 out=res[m][:, OT * h : OT * (h + 1)].rearrange("p (c t) -> p c t", t=TR),
@@ -280,10 +289,11 @@ def tile_snnlayer_pa_kernel(
                 op1=ALU.mult,
             )
 
-        def finish(m):
-            sl = slice(2 * OT * m, 2 * OT * (m + 1))
-            nc.vector.tensor_tensor(out=res[m][:], in0=res[m][:], in1=b_sb[:, sl], op=ALU.add)
-            nc.sync.dma_start(out=out[:, sl], in_=res[m][:])
+        def finish(n0, n1):
+            sl = slice(OT * n0, OT * n1)
+            r = res[n0 // 2][:, OT * (n0 % 2) : OT * (n0 % 2 + n1 - n0)]
+            nc.vector.tensor_tensor(out=r, in0=r, in1=b_sb[:, sl], op=ALU.add)
+            nc.sync.dma_start(out=out[:, sl], in_=r)
 
         def next_fill():
             if fill:
@@ -291,35 +301,57 @@ def tile_snnlayer_pa_kernel(
 
         next_load = NBUF_W
         pending = []
-        for r in range(N_CHUNK + LAG_M + 1):
-            if r < N_CHUNK:
-                for item in transposes(r):
-                    copy_out(item, False)
+        for r in range(LAST):
+            for g in range(PASSES_W):
+                transposes(r, g)
+                copy_out(r, g)
             if r < 3:
                 act_bank(2 * r)
                 act_bank(2 * r + 1)
+            if r in MB_ROUND:
+                mem_minus_bias(MB_ROUND.index(r))
             if r < 4:
                 taus(r)
             if 1 <= r < 4:
                 act_quant(r - 1)
-            if FILL_FROM <= r <= FILL_TWO:
-                next_fill()
-            rq = r - LAG_Q
-            if 0 <= rq < N_CHUNK:
-                quant(rq)
+            if r >= 1:
+                quant(r - 1)
             for n in pending:
                 scale_sums(n)
-            if FILL_FROM <= r:
+            if r >= FILL_FROM:
                 next_fill()
             for n in pending:
                 if n % 2 == 1:
-                    finish(n // 2)
+                    finish(n - 1, n + 1)
+            if FILL_FROM <= r and r % 2 == 0:
+                next_fill()
+            if r in MB_ROUND:
+                mb_v[MB_ROUND.index(r)]()
             pending = []
             rm = r - LAG_M
-            if 0 <= rm < N_CHUNK:
+            if rm >= 0:
                 mx(rm)
                 if rm % N_W == N_W - 1:
                     pending.append(rm // N_W)
-            if r < N_CHUNK and next_load < N_CHUNK:
-                load_w(next_load)
+            if next_load < N_CHUNK:
+                load_w(next_load, LAST_PARTS if next_load == LAST else 1)
                 next_load += 1
+
+        mx(LAST - 3)
+        for g in range(PASSES_W):
+            transposes(LAST, g)
+            copy_out(LAST, g)
+            if g == 1:
+                mx(LAST - 2)
+        scale_sums(N_OT - 2)
+        finish(N_OT - 2, N_OT - 1)
+        quant(LAST - 1)
+        mx(LAST - 1)
+        while fill:
+            next_fill()
+        quant(LAST, 0, 2)
+        quant(LAST, 2, 3)
+        quant(LAST, 3, 4)
+        mx(LAST)
+        scale_sums(N_OT - 1)
+        finish(N_OT - 1, N_OT)

@@ -184,22 +184,21 @@ def tile_snnlayer_pa_kernel(
             s = spk_sb[:, KDIM + FW * f : KDIM + FW * (f + 1)]
             box = {}
 
-            def w0():
-                box["t1"] = tpool.tile([P, FW], F32, name="t1_%d" % f, tag="t1")
-                nc.vector.tensor_tensor(out=box["t1"][:], in0=bt_sb[:, sl], in1=s, op=ALU.subtract)
+            def mb():
+                nc.vector.tensor_tensor(out=b_sb[:, sl], in0=xbank[f][:], in1=a3_sb[:, sl], op=ALU.mult)
 
             def b1():
                 nc.vector.tensor_tensor(out=b_sb[:, sl], in0=mem_sb[:, sl], in1=b_sb[:, sl], op=ALU.subtract)
 
             def w1():
-                nc.vector.tensor_tensor(out=box["t1"][:], in0=box["t1"][:], in1=p_sb[:, sl], op=ALU.mult)
+                box["t1"] = tpool.tile([P, FW], F32, name="t1_%d" % f, tag="t1")
+                nc.vector.scalar_tensor_tensor(
+                    out=box["t1"][:], in0=bt_sb[:, sl], scalar=-1.0, in1=p_sb[:, sl], op0=ALU.add, op1=ALU.mult
+                )
 
             def w2():
-                nc.vector.tensor_tensor(out=box["t1"][:], in0=box["t1"][:], in1=s, op=ALU.add)
-
-            def w3():
                 nc.vector.scalar_tensor_tensor(
-                    out=box["t1"][:], in0=box["t1"][:], scalar=KAPPA, in1=s, op0=ALU.add, op1=ALU.mult
+                    out=box["t1"][:], in0=box["t1"][:], scalar=1.0 + KAPPA, in1=s, op0=ALU.add, op1=ALU.mult
                 )
 
             def b2():
@@ -207,11 +206,8 @@ def tile_snnlayer_pa_kernel(
                     out=b_sb[:, sl], in0=box["t1"][:], scalar=-1.8, in1=b_sb[:, sl], op0=ALU.mult, op1=ALU.add
                 )
 
-            def mb():
-                nc.vector.tensor_tensor(out=b_sb[:, sl], in0=xbank[f][:], in1=a3_sb[:, sl], op=ALU.mult)
-
             mb_v.append(mb)
-            return [b1, w0, w1, w2, w3, b2]
+            return [w1, b1, w2, b2]
 
         fill = []
         mb_v = []
@@ -323,8 +319,6 @@ def tile_snnlayer_pa_kernel(
             for n in pending:
                 if n % 2 == 1:
                     finish(n - 1, n + 1)
-            if FILL_FROM <= r and r % 2 == 0:
-                next_fill()
             if r in MB_ROUND:
                 mb_v[MB_ROUND.index(r)]()
             pending = []

@@ -24,9 +24,8 @@ N_CHUNK = N_OT * N_W
 FW = 512
 FLOPS = 2 * 128 * 3 * KDIM * ODIM
 
-MANUAL = True
 LAG_M = 3
-LAST_PARTS = 4
+LAST_PARTS = 2
 NBUF_W = 10
 GB = 6
 FILL_FROM = 5
@@ -53,8 +52,7 @@ def tile_snnlayer_pa_kernel(
     nc = tc.nc
     weights = [W_rec4in, W_out2in, W_x2in]
     with ExitStack() as ctx:
-        if MANUAL:
-            ctx.enter_context(tc.manual_schedule())
+        ctx.enter_context(tc.manual_schedule())
         keep = ctx.enter_context(tc.tile_pool(name="keep", bufs=1))
         wpool = ctx.enter_context(tc.tile_pool(name="wraw", bufs=NBUF_W))
         gpool = ctx.enter_context(tc.tile_pool(name="grp", bufs=GB))
@@ -105,7 +103,7 @@ def tile_snnlayer_pa_kernel(
                     in_=weights[w][OT * n : OT * (n + 1), ks].rearrange("(c t) k -> c t k", t=TR),
                 )
 
-        load_w(0, 2)
+        load_w(0)
         nc.sync.dma_start(out=spk_sb[:, KDIM:], in_=spk_t[:, KDIM:])
         load_w(1)
         nc.sync.dma_start(out=spk_sb[:, :KDIM], in_=spk_t[:, :KDIM])

@@ -268,6 +268,7 @@ def tile_snnlayer_pa_kernel(
                 )
 
         res = {}
+        stores = []
 
         def scale_sums(n):
             m, h = divmod(n, 2)
@@ -287,7 +288,12 @@ def tile_snnlayer_pa_kernel(
             sl = slice(OT * n0, OT * n1)
             r = res[n0 // 2][:, OT * (n0 % 2) : OT * (n0 % 2 + n1 - n0)]
             nc.vector.tensor_tensor(out=r, in0=r, in1=b_sb[:, sl], op=ALU.add)
-            nc.sync.dma_start(out=out[:, sl], in_=r)
+            stores.append((sl, r))
+
+        def store_all():
+            for sl, r in stores:
+                nc.sync.dma_start(out=out[:, sl], in_=r)
+            stores.clear()
 
         def next_fill():
             if fill:
@@ -325,6 +331,8 @@ def tile_snnlayer_pa_kernel(
                 mx(rm)
                 if rm % N_W == N_W - 1:
                     pending.append(rm // N_W)
+            if next_load == N_CHUNK:
+                store_all()
             if next_load < N_CHUNK:
                 load_w(next_load, LAST_PARTS if next_load == LAST else 1)
                 next_load += 1
@@ -337,6 +345,7 @@ def tile_snnlayer_pa_kernel(
                 mx(LAST - 2)
         scale_sums(N_OT - 2)
         finish(N_OT - 2, N_OT - 1)
+        store_all()
         quant(LAST - 1)
         mx(LAST - 1)
         while fill:
@@ -347,3 +356,4 @@ def tile_snnlayer_pa_kernel(
         mx(LAST)
         scale_sums(N_OT - 1)
         finish(N_OT - 1, N_OT)
+        store_all()

from contextlib import ExitStack

import concourse.mybir as mybir
from concourse.masks import make_identity

F32 = mybir.dt.float32
BF16 = mybir.dt.bfloat16
U32 = mybir.dt.uint32
U8 = mybir.dt.uint8
I32 = mybir.dt.int32
FP8X4 = mybir.dt.float8_e4m3fn_x4
ALU = mybir.AluOpType
ACT = mybir.ActivationFunctionType

P = 128
KDIM = 2048
ODIM = 2048
OT = 256
TR = OT // P
N_OT = ODIM // OT
N_W = 3
PASSES_W = KDIM // 512
N_CHUNK = N_OT * N_W
FW = 512
FLOPS = 2 * 128 * 3 * KDIM * ODIM

LAG_M = 3
LAST_PARTS = 2
NBUF_W = 10
GB = 6
FILL_FROM = 5
MB_ROUND = [4, 8, 12, 16]
KAPPA = 0.1 / 1.8


def tile_snnlayer_pa_kernel(
    tc,
    x_t,
    spk_t,
    mem_t_in,
    b_t_in,
    W_x2in,
    b_x2in,
    W_rec4in,
    b_rec4in,
    W_out2in,
    b_out2in,
    tau_adp_in,
    tau_m_in,
    out,
):
    nc = tc.nc
    weights = [W_rec4in, W_out2in, W_x2in]
    with ExitStack() as ctx:
        ctx.enter_context(tc.manual_schedule())
        keep = ctx.enter_context(tc.tile_pool(name="keep", bufs=1))
        wpool = ctx.enter_context(tc.tile_pool(name="wraw", bufs=NBUF_W))
        gpool = ctx.enter_context(tc.tile_pool(name="grp", bufs=GB))
        tpool = ctx.enter_context(tc.tile_pool(name="tmp", bufs=2))
        psum = ctx.enter_context(tc.psum_pool(name="psum", bufs=1))

        warm = keep.tile([P, 2], F32, name="warm")
        nc.vector.memset(warm[:], 0.0)
        nc.scalar.activation(out=warm[:, 1:2], in_=warm[:, 0:1], func=ACT.Sigmoid)
        vrow = keep.tile([P, ODIM], BF16, name="vrow")
        nc.vector.memset(vrow[:].bitcast(I32), 0)
        sel = keep.tile([P, 3, P], BF16, name="sel")
        nc.vector.memset(sel[:].bitcast(I32), 0)
        nc.vector.memset(sel[0:3, 0, :], -3.0)
        nc.vector.memset(sel[32:33, 1, :], 1.0)
        nc.vector.memset(sel[64:65, 2, :], 1.0)
        ident = keep.tile([P, P], F32, name="ident")
        make_identity(nc, ident[:])
        identb = keep.tile([P, P], BF16, name="identb")
        make_identity(nc, identb[:])

        def row(v):
            return v.rearrange("(o n) -> o n", o=1)

        nc.scalar.dma_start(out=vrow[32:33, :], in_=row(tau_m_in))
        nc.scalar.dma_start(out=vrow[64:65, :], in_=row(tau_adp_in))
        nc.scalar.dma_start(out=vrow[0:1, :], in_=row(b_x2in))
        nc.scalar.dma_start(out=vrow[1:2, :], in_=row(b_rec4in))
        nc.scalar.dma_start(out=vrow[2:3, :], in_=row(b_out2in))

        spk_sb = keep.tile([P, 2 * KDIM], BF16, name="spk_sb")
        bt_sb = keep.tile([P, ODIM], BF16, name="bt_sb")
        mem_sb = keep.tile([P, ODIM], BF16, name="mem_sb")
        x_sb = keep.tile([P, KDIM], BF16, name="x_sb")

        wraw = {}

        LAST = N_CHUNK - 1

        def load_w(ci, parts=1):
            n, w = divmod(ci, N_W)
            t = wpool.tile([P, TR, KDIM], BF16, name="wraw%d" % ci, tag="wraw")
            wraw[ci] = t
            for h in range(parts):
                ks = slice(KDIM // parts * h, KDIM // parts * (h + 1))
                nc.sync.dma_start(
                    out=t[:, :, ks],
                    in_=weights[w][OT * n : OT * (n + 1), ks].rearrange("(c t) k -> c t k", t=TR),
                )

        load_w(0)
        nc.sync.dma_start(out=spk_sb[:, KDIM:], in_=spk_t[:, KDIM:])
        load_w(1)
        nc.sync.dma_start(out=spk_sb[:, :KDIM], in_=spk_t[:, :KDIM])
        load_w(2)
        nc.sync.dma_start(out=x_sb[:], in_=x_t)
        load_w(3)
        nc.sync.dma_start(out=mem_sb[:], in_=mem_t_in)
        load_w(4)
        nc.sync.dma_start(out=bt_sb[:], in_=b_t_in)
        for ci in range(5, NBUF_W):
            load_w(ci)

        p_sb = keep.tile([P, ODIM], F32, name="p_sb")
        a3_sb = keep.tile([P, ODIM], F32, name="a3_sb")
        b_sb = keep.tile([P, ODIM], F32, name="b_sb")

        def bank(name):
            return psum.tile([P, 512], F32, name=name, tag="tp", bufs=6)

        def taus(f):
            sl = slice(FW * f, FW * (f + 1))
            tm = bank("tm%d" % f)
            nc.tensor.matmul(tm[:], lhsT=sel[:, 1, :], rhs=vrow[:, sl], start=True, stop=True)
            nc.scalar.activation(out=a3_sb[:, sl], in_=tm[:], func=ACT.Sigmoid, scale=-1.0)
            tq = bank("tq%d" % f)
            nc.tensor.matmul(tq[:], lhsT=sel[:, 2, :], rhs=vrow[:, sl], start=True, stop=True)
            nc.scalar.activation(out=p_sb[:, sl], in_=tq[:], func=ACT.Sigmoid)

        xbank = {}

        def mem_minus_bias(f):
            sl = slice(FW * f, FW * (f + 1))
            xb = bank("xb%d" % f)
            nc.tensor.matmul(xb[:], lhsT=sel[:, 0, :], rhs=vrow[:, sl], start=True, stop=False)
            nc.tensor.matmul(xb[:], lhsT=identb[:], rhs=mem_sb[:, sl], start=False, stop=True)
            xbank[f] = xb

        a_grp = keep.tile([P, 12 * 512], BF16, name="a_grp", align_bytes=64)
        a_codes = keep.tile([P, 12 * P], U32, name="a_codes", align_bytes=64)
        a_scales = keep.tile([P, 12 * P], U8, name="a_scales", align_bytes=64)
        x_w = x_sb[:].bitcast(F32)
        spk_w = spk_sb[:].bitcast(F32)
        a_grp_w = a_grp[:].bitcast(F32).rearrange("p (a b u) -> p a b u", b=P, u=2)

        def act_words(a):
            w, g = divmod(a, PASSES_W)
            if w == 0:
                return spk_w, 1024 + 256 * g
            if w == 1:
                return spk_w, 256 * g
            return x_w, 256 * g

        def act_bank(i):
            bk = bank("ab%d" % i)
            for j in range(2):
                src, off = act_words(2 * i + j)
                for u in range(2):
                    q = 2 * j + u
                    nc.tensor.transpose(
                        bk[:, P * q : P * (q + 1)], src[:, off + P * u : off + P * (u + 1)], ident[:]
                    )
            nc.vector.tensor_copy(
                out=a_grp_w[:, 2 * i : 2 * i + 2, :, :],
                in_=bk[:].rearrange("p (a u b) -> p a b u", a=2, u=2),
            )

        def act_quant(w):
            nc.vector.quantize_mx(
                out=a_codes[:, 512 * w : 512 * (w + 1)].bitcast(FP8X4),
                scales=a_scales[:, 512 * w : 512 * (w + 1)],
                in_=a_grp[:, 2048 * w : 2048 * (w + 1)],
            )

        def bterm(f):
            sl = slice(FW * f, FW * (f + 1))
            s = spk_sb[:, KDIM + FW * f : KDIM + FW * (f + 1)]
            box = {}

            def mb():
                nc.vector.tensor_tensor(out=b_sb[:, sl], in0=xbank[f][:], in1=a3_sb[:, sl], op=ALU.mult)

            def b1():
                nc.vector.tensor_tensor(out=b_sb[:, sl], in0=mem_sb[:, sl], in1=b_sb[:, sl], op=ALU.subtract)

            def w1():
                box["t1"] = tpool.tile([P, FW], F32, name="t1_%d" % f, tag="t1")
                nc.vector.scalar_tensor_tensor(
                    out=box["t1"][:], in0=bt_sb[:, sl], scalar=-1.0, in1=p_sb[:, sl], op0=ALU.add, op1=ALU.mult
                )

            def w2():
                nc.vector.scalar_tensor_tensor(
                    out=box["t1"][:], in0=box["t1"][:], scalar=1.0 + KAPPA, in1=s, op0=ALU.add, op1=ALU.mult
                )

            def b2():
                nc.vector.scalar_tensor_tensor(
                    out=b_sb[:, sl], in0=box["t1"][:], scalar=-1.8, in1=b_sb[:, sl], op0=ALU.mult, op1=ALU.add
                )

            mb_v.append(mb)
            return [w1, b1, w2, b2]

        fill = []
        mb_v = []
        for f in range(ODIM // FW):
            fill.extend(bterm(f))

        grp = {}
        codes = {}
        scales = {}
        acc = {}

        wbank = {}

        def transposes(ci, g):
            ww = wraw[ci][:].bitcast(F32)
            bk = bank("wb%d_%d" % (ci, g))
            for u in range(2):
                for tt in range(TR):
                    col = 256 * u + P * tt
                    off = 256 * g + P * u
                    nc.tensor.transpose(bk[:, col : col + P], ww[:, tt, off : off + P], ident[:])
            wbank[ci, g] = bk

        def copy_out(ci, g):
            if ci not in grp:
                gt = gpool.tile([P, 4096], BF16, name="grp%d" % ci, tag="grp", bufs=4, align_bytes=64)
                grp[ci] = gt
            gw = grp[ci][:].bitcast(F32).rearrange("p (j u) -> p j u", u=2)
            dst = gw[:, 256 * g : 256 * (g + 1), :]
            src = wbank[ci, g][:].rearrange("p (u j) -> p j u", u=2)
            nc.scalar.copy(out=dst, in_=src)

        def quant(ci, g0=0, g1=PASSES_W):
            if ci not in codes:
                cd = gpool.tile([P, 1024], U32, name="cd%d" % ci, tag="cd", align_bytes=64)
                sc = gpool.tile([P, 1024], U8, name="sc%d" % ci, tag="sc", align_bytes=64)
                codes[ci] = cd
                scales[ci] = sc
            ws = slice(256 * g0, 256 * g1)
            nc.vector.quantize_mx(
                out=codes[ci][:, ws].bitcast(FP8X4),
                scales=scales[ci][:, ws],
                in_=grp[ci][:, 1024 * g0 : 1024 * g1],
            )

        def mx(ci):
            n, w = divmod(ci, N_W)
            if w == 0:
                acc[n] = psum.tile([P, OT], F32, name="acc%d" % n, tag="acc", bufs=2)
            for g in range(PASSES_W):
                r = w * PASSES_W + g
                nc.tensor.matmul_mx(
                    out=acc[n][:],
                    lhsT=a_codes[:, P * r : P * (r + 1)].bitcast(FP8X4),
                    lhsT_scale=a_scales[:, P * r : P * (r + 1)],
                    rhs=codes[ci][:, 256 * g : 256 * (g + 1)].bitcast(FP8X4),
                    rhs_scale=scales[ci][:, 256 * g : 256 * (g + 1)],
                    start=(r == 0),
                    stop=(r == N_W * PASSES_W - 1),
                )

        res = {}
        stores = []

        def scale_sums(n):
            m, h = divmod(n, 2)
            if h == 0:
                res[m] = tpool.tile([P, 2 * OT], F32, name="res%d" % m, tag="res", bufs=4)
            sl = slice(OT * n, OT * (n + 1))
            nc.vector.scalar_tensor_tensor(
                out=res[m][:, OT * h : OT * (h + 1)].rearrange("p (c t) -> p c t", t=TR),
                in0=acc[n][:].rearrange("p (t c) -> p c t", t=TR),
                scalar=3.0,
                in1=a3_sb[:, sl].rearrange("p (c t) -> p c t", t=TR),
                op0=ALU.mult,
                op1=ALU.mult,
            )

        def finish(n0, n1):
            sl = slice(OT * n0, OT * n1)
            r = res[n0 // 2][:, OT * (n0 % 2) : OT * (n0 % 2 + n1 - n0)]
            nc.vector.tensor_tensor(out=r, in0=r, in1=b_sb[:, sl], op=ALU.add)
            stores.append((sl, r))

        def store_all():
            for sl, r in stores:
                nc.sync.dma_start(out=out[:, sl], in_=r)
            stores.clear()

        def next_fill():
            if fill:
                fill.pop(0)()

        next_load = NBUF_W
        pending = []
        for r in range(LAST):
            for g in range(PASSES_W):
                transposes(r, g)
                copy_out(r, g)
            if r < 3:
                act_bank(2 * r)
                act_bank(2 * r + 1)
            if r in MB_ROUND:
                mem_minus_bias(MB_ROUND.index(r))
            if r < 4:
                taus(r)
            if 1 <= r < 4:
                act_quant(r - 1)
            if r >= 1:
                quant(r - 1)
            for n in pending:
                scale_sums(n)
            if r >= FILL_FROM:
                next_fill()
            for n in pending:
                if n % 2 == 1:
                    finish(n - 1, n + 1)
            if r in MB_ROUND:
                mb_v[MB_ROUND.index(r)]()
            pending = []
            rm = r - LAG_M
            if rm >= 0:
                mx(rm)
                if rm % N_W == N_W - 1:
                    pending.append(rm // N_W)
            if next_load == N_CHUNK:
                store_all()
            if next_load < N_CHUNK:
                load_w(next_load, LAST_PARTS if next_load == LAST else 1)
                next_load += 1

        mx(LAST - 3)
        for g in range(PASSES_W):
            transposes(LAST, g)
            copy_out(LAST, g)
            if g == 1:
                mx(LAST - 2)
        scale_sums(N_OT - 2)
        finish(N_OT - 2, N_OT - 1)
        store_all()
        quant(LAST - 1)
        mx(LAST - 1)
        while fill:
            next_fill()
        quant(LAST, 0, 2)
        quant(LAST, 2, 3)
        quant(LAST, 3, 4)
        mx(LAST)
        scale_sums(N_OT - 1)
        finish(N_OT - 1, N_OT)
        store_all()
